import numpy as np
import ml_dtypes


def mxq(x, axis, fmt="e4m3"):
    dtype, down = {"e4m3": (ml_dtypes.float8_e4m3fn, 7), "e5m2": (ml_dtypes.float8_e5m2, 14)}[fmt]
    v = np.moveaxis(np.asarray(x, np.float32).astype(ml_dtypes.bfloat16).astype(np.float64), axis, -1)
    blocks = v.reshape(v.shape[:-1] + (-1, 32))
    amax = np.abs(blocks).max(-1, keepdims=True)
    byte = np.maximum(np.where(amax > 0, np.frexp(amax)[1] - 1 + 127, 0) - down, 1)
    scale = np.exp2(byte - 127.0)
    codes = (blocks / scale).astype(np.float32).astype(dtype).astype(np.float64)
    return np.moveaxis((codes * scale).reshape(v.shape), -1, axis)


WIDE = False


def mx_kscale(k):
    if not WIDE:
        return np.ones(k)
    levels = np.array([10, -10, 5, -5, 0])
    if k % 512:
        return np.exp2(np.random.permutation(np.resize(levels, k // 32))).repeat(32)
    a = np.empty((k // 512, 16))
    for p in range(k // 512):
        a[p, :8] = np.random.permutation(np.resize(levels, 8))
        for g in range(8):
            far = levels[np.abs(levels - a[p, g]) >= 10]
            a[p, g + 8] = far[np.random.randint(len(far))]
    return np.exp2(a.ravel()).repeat(32)


BF16 = ml_dtypes.bfloat16


def bf(x):
    return np.asarray(x, np.float32).astype(BF16)


def f64(x):
    return np.asarray(x).astype(np.float64)


B, T, D, H, HD = 2, 512, 1024, 8, 128
E = H * HD
HALF = HD // 2


def rotate_half(u):
    return np.concatenate((-u[..., HALF:], u[..., :HALF]), axis=-1)


def draw0():
    s = mx_kscale(D)
    return {"x": bf(np.random.standard_normal((B, T, D)) * s),
            "rope_cos": bf(np.random.random_sample((1, 1, T, HD))),
            "rope_sin": bf(np.random.random_sample((1, 1, T, HD))),
            "qkv_w": bf(np.random.standard_normal((3 * E, D)) / np.sqrt(D) / s[None, :]),
            "qkv_b": bf(np.random.standard_normal(3 * E) * 0.3)}


def core(x, rope_cos, rope_sin, qkv_w, qkv_b):
    qkv = (mxq(f64(x), 2, "e4m3") @ mxq(f64(qkv_w), 1, "e4m3").T) + f64(qkv_b)
    qkv = qkv.reshape(B, T, 3, H, HD).transpose(2, 0, 3, 1, 4)
    q, k, v = qkv[0], qkv[1], qkv[2]
    cos = f64(rope_cos)[:, :, :T, :]
    sin = f64(rope_sin)[:, :, :T, :]
    q_rot = q * cos + rotate_half(q) * sin
    k_rot = k * cos + rotate_half(k) * sin
    return q_rot, k_rot, v


def e4m3fn_bytes(y):
    return np.clip(np.asarray(y, np.float64), -448.0, 448.0).astype(np.float32).astype(ml_dtypes.float8_e4m3fn).view(np.uint8)


def e4m3fn_values(b):
    return np.asarray(b, np.uint8).view(ml_dtypes.float8_e4m3fn).astype(np.float64)


def setup_inputs():
    d = draw0()
    x0 = np.asarray(d['qkv_w']).astype(np.float64)
    s = (np.max(np.abs(x0), axis=(0,), keepdims=True) / 448.0).astype(np.float32)
    out = {}
    for k, v in d.items():
        if k == 'qkv_w':
            out['qkv_w_bytes'] = e4m3fn_bytes(x0 / s.astype(np.float64))
            out['qkv_w_scale'] = s
        else:
            out[k] = v
    return out


def reference(x, rope_cos, rope_sin, qkv_w_bytes, qkv_w_scale, qkv_b):
    return core(x, rope_cos, rope_sin, e4m3fn_values(qkv_w_bytes) * qkv_w_scale.astype(np.float64), qkv_b)

@@ -1,0 +1,263 @@
+from contextlib import ExitStack
+
+import concourse.mybir as mybir
+from concourse.masks import make_identity
+
+B, T, D, H, HD = 2, 512, 1024, 8, 128
+FLOPS = 2 * B * T * D * 3 * H * HD
+
+F32 = mybir.dt.float32
+BF16 = mybir.dt.bfloat16
+U32 = mybir.dt.uint32
+U8 = mybir.dt.uint8
+FP8 = mybir.dt.float8_e4m3fn
+FP8X4 = mybir.dt.float8_e4m3fn_x4
+ADD = mybir.AluOpType.add
+MULT = mybir.AluOpType.mult
+COPY = mybir.ActivationFunctionType.Copy
+
+P = 128
+G = D // 512
+TB = T // P
+NH = 3 * H
+ON_VECTOR = 3
+
+
+def tile_causalselfattention_pa_kernel(
+    tc, x, rope_cos, rope_sin, qkv_w_bytes, qkv_w_scale, qkv_b, out_0, out_1, out_2
+):
+    nc = tc.nc
+    outs = (out_0, out_1, out_2)
+    order = [(j, h) for h in range(H) for j in range(3)]
+
+    with ExitStack() as ctx:
+        keep = ctx.enter_context(tc.tile_pool(name="keep", bufs=1))
+        work = ctx.enter_context(tc.tile_pool(name="work", bufs=3))
+        psum = ctx.enter_context(tc.psum_pool(name="psum", bufs=2))
+        ctx.enter_context(tc.manual_schedule(engines={mybir.EngineType.PE}))
+
+        ident = keep.tile([P, P], F32, name="ident")
+        make_identity(nc, ident[:])
+        perm = keep.tile([P, P], F32, name="perm")
+        nc.vector.tensor_copy(out=perm[:, 0:64], in_=ident[:, 64:128])
+        nc.vector.tensor_copy(out=perm[:, 64:128], in_=ident[:, 0:64])
+        b_rows = keep.tile([P, P], BF16, name="b_rows")
+        nc.vector.memset(b_rows[:], 0.0)
+
+        sc_b = keep.tile([P, D], F32, name="sc_b")
+        nc.sync.dma_start(out=sc_b[:], in_=qkv_w_scale.rearrange("o k -> (o k)").partition_broadcast(P))
+        w_view = qkv_w_bytes.rearrange("(j h p) k -> h p j k", j=3, h=H, p=P)
+        wbytes = [keep.tile([P, 3, D], U8, name="wbytes%d" % h) for h in range(H)]
+        nc.sync.dma_start(out=wbytes[0][:], in_=w_view[0])
+        x_sb = [keep.tile([P, TB, D], BF16, name="x_sb%d" % b) for b in range(B)]
+        cos_sb = keep.tile([P, TB, HD], BF16, name="cos_sb")
+        sin_sb = keep.tile([P, TB, HD], BF16, name="sin_sb")
+        bv = keep.tile([P, H * HD], BF16, name="bv")
+        for b in range(B):
+            xv = x[b].rearrange("(p t) k -> p t k", t=TB)
+            for t in range(TB):
+                nc.sync.dma_start(out=x_sb[b][:, t, :], in_=xv[:, t, :])
+        nc.sync.dma_start(out=cos_sb[:], in_=rope_cos[0, 0].rearrange("(p t) d -> p t d", t=TB))
+        nc.sync.dma_start(out=sin_sb[:], in_=rope_sin[0, 0].rearrange("(p t) d -> p t d", t=TB))
+        nc.sync.dma_start(out=b_rows[0:NH, :], in_=qkv_b.rearrange("(r d) -> r d", d=HD))
+        nc.sync.dma_start(out=wbytes[1][:], in_=w_view[1])
+        nc.sync.dma_start(out=bv[:], in_=qkv_b[2 * H * HD : 3 * H * HD].partition_broadcast(P))
+        for h in range(2, H):
+            nc.sync.dma_start(out=wbytes[h][:], in_=w_view[h])
+
+        xc = keep.tile([P, G, B, T], U32, name="xc", align_bytes=64)
+        xs = keep.tile([P, G, B, T], U8, name="xs", align_bytes=64)
+        wc = keep.tile([P, NH, G * P], U32, name="wc", align_bytes=64)
+        ws = keep.tile([P, NH, G * P], U8, name="ws", align_bytes=64)
+
+        def bank(tag):
+            return psum.tile([P, TB, P], F32, name=tag, tag=tag, bufs=(4 if tag == "acc" else 2))
+
+        def turn(words, sorted_words, name, tag, on_vector):
+            tp = bank(tag)
+            for g in range(G):
+                for u in range(2):
+                    n = 2 * g + u
+                    picked = words[:, P * n : P * (n + 1)] if sorted_words else words[:, 256 * g + u : 256 * (g + 1) : 2]
+                    nc.tensor.transpose(tp[:, n, :], picked, ident[:])
+            grouped = work.tile([P, G * 512], BF16, name=name, tag=name, bufs=3, align_bytes=64)
+            dst = grouped[:].bitcast(F32).rearrange("p (g r u) -> p g r u", g=G, u=2)
+            src = tp[:].rearrange("p (g u) r -> p g r u", g=G)
+            if on_vector:
+                nc.vector.tensor_copy(out=dst, in_=src)
+            else:
+                nc.scalar.copy(out=dst, in_=src)
+            return grouped
+
+        wb_t = {}
+        wg_t = {}
+        acc_t = {}
+        ar_t = {}
+
+        def stage_a(i):
+            j, h = order[i]
+            codes = wbytes[h][:, j, :].bitcast(FP8)
+            wb = work.tile([P, D], BF16, name="wb", tag="wb", bufs=4, align_bytes=64)
+            if i < ON_VECTOR:
+                nc.vector.tensor_tensor(out=wb[:], in0=codes, in1=sc_b[:], op=MULT)
+            else:
+                wf = work.tile([P, D], BF16, name="wf", tag="wf", bufs=3)
+                nc.scalar.copy(out=wf[:], in_=codes)
+                for g in range(G):
+                    ks = slice(g * 512, (g + 1) * 512)
+                    nc.gpsimd.tensor_tensor(
+                        out=wb[:, ks].rearrange("p (u q e) -> p u q e", u=2, e=2),
+                        in0=wf[:, ks].rearrange("p (q u e) -> p u q e", u=2, e=2),
+                        in1=sc_p[:, ks].rearrange("p (u q e) -> p u q e", u=2, e=2),
+                        op=MULT,
+                    )
+            wb_t[i] = wb
+
+        def stage_b(i):
+            wg_t[i] = turn(wb_t[i][:].bitcast(F32), i >= ON_VECTOR, "wg", "tp", False)
+
+        def stage_c(i):
+            nc.vector.quantize_mx(out=wc[:, i, :].bitcast(FP8X4), scales=ws[:, i, :], in_=wg_t[i][:])
+
+        def stage_d(i):
+            j, h = order[i]
+            for b in range(B):
+                acc = bank("acc")
+                if j == 2:
+                    for t in range(TB):
+                        toks = slice(t * P, (t + 1) * P)
+                        for g in range(G):
+                            cols = slice(g * P, (g + 1) * P)
+                            nc.tensor.matmul_mx(
+                                out=acc[:, t, :],
+                                lhsT=xc[:, g, b, toks].bitcast(FP8X4),
+                                lhsT_scale=xs[:, g, b, toks],
+                                rhs=wc[:, i, cols].bitcast(FP8X4),
+                                rhs_scale=ws[:, i, cols],
+                                start=(g == 0),
+                                stop=(g == G - 1),
+                            )
+                else:
+                    for g in range(G):
+                        cols = slice(g * P, (g + 1) * P)
+                        nc.tensor.matmul_mx(
+                            out=acc[:].rearrange("p t r -> p (t r)"),
+                            lhsT=wc[:, i, cols].bitcast(FP8X4),
+                            lhsT_scale=ws[:, i, cols],
+                            rhs=xc[:, g, b, :].bitcast(FP8X4),
+                            rhs_scale=xs[:, g, b, :],
+                            start=(g == 0),
+                            stop=(g == G - 1),
+                        )
+                acc_t[(i, b)] = acc
+
+        def store(j, h, b, o_sb):
+            nc.sync.dma_start(out=outs[j][b, h].rearrange("(p t) d -> p (t d)", t=TB), in_=o_sb)
+
+        def stage_e(i):
+            j, h = order[i]
+            for b in range(B):
+                acc = acc_t[(i, b)]
+                if j == 2:
+                    o_sb = work.tile([P, TB, HD], F32, name="o_sb", tag="o_sb", bufs=4)
+                    nc.vector.tensor_tensor(
+                        out=o_sb[:],
+                        in0=acc[:],
+                        in1=bv[:, h * HD : (h + 1) * HD].unsqueeze(1).to_broadcast([P, TB, HD]),
+                        op=ADD,
+                    )
+                    store(j, h, b, o_sb[:].rearrange("p t d -> p (t d)"))
+                else:
+                    ar = work.tile([P, 2, T], F32, name="ar", tag="ar", bufs=4)
+                    nc.vector.scalar_tensor_tensor(
+                        out=ar[:],
+                        in0=acc[:].rearrange("p t r -> p (t r)").unsqueeze(1).to_broadcast([P, 2, T]),
+                        scalar=bcol[:, j * H + h : j * H + h + 1],
+                        in1=tab[:],
+                        op0=ADD,
+                        op1=MULT,
+                    )
+                    ar_t[(i, b)] = ar
+
+        def stage_f(i):
+            j, h = order[i]
+            if j == 2:
+                return
+            for b in range(B):
+                ar = ar_t[(i, b)]
+                ot = bank("ot")
+                for t in range(TB):
+                    cols = slice(t * P, (t + 1) * P)
+                    nc.tensor.matmul(ot[:, t, :], lhsT=ar[:, 0, cols], rhs=ident[:], start=True, stop=False, is_transpose=True)
+                    nc.tensor.matmul(ot[:, t, :], lhsT=ar[:, 1, cols], rhs=perm[:], start=False, stop=True, is_transpose=True)
+                o_sb = work.tile([P, TB, HD], F32, name="o_sb", tag="o_sb", bufs=4)
+                nc.scalar.copy(out=o_sb[:], in_=ot[:])
+                store(j, h, b, o_sb[:].rearrange("p t d -> p (t d)"))
+
+        cos_f = keep.tile([P, TB, HD], F32, name="cos_f")
+        sin_p = keep.tile([P, TB, HD], F32, name="sin_p")
+        b_f = keep.tile([P, P], F32, name="b_f")
+        tab = keep.tile([P, 2, T], F32, name="tab")
+        bcol = keep.tile([P, P], F32, name="bcol")
+
+        def tables():
+            nc.scalar.copy(out=cos_f[:], in_=cos_sb[:])
+            nc.scalar.copy(out=sin_p[:, :, 0:64], in_=sin_sb[:, :, 64:128])
+            nc.scalar.activation(out=sin_p[:, :, 64:128], in_=sin_sb[:, :, 0:64], func=COPY, scale=-1.0)
+            nc.scalar.copy(out=b_f[:], in_=b_rows[:])
+            for n, src in enumerate((cos_f, sin_p)):
+                tp = bank("tp")
+                for t in range(TB):
+                    nc.tensor.transpose(tp[:, t, :], src[:, t, :], ident[:])
+                nc.scalar.copy(out=tab[:, n, :], in_=tp[:].rearrange("p t r -> p (t r)"))
+            tp = bank("tp")
+            nc.tensor.transpose(tp[:, 0, :], b_f[:], ident[:])
+            nc.scalar.copy(out=bcol[:], in_=tp[:, 0, :])
+
+        for i in range(ON_VECTOR):
+            stage_a(i)
+        sc_p = keep.tile([P, D], F32, name="sc_p")
+        for g in range(G):
+            ks = slice(g * 512, (g + 1) * 512)
+            nc.vector.tensor_copy(
+                out=sc_p[:, ks].rearrange("p (u q e) -> p u q e", u=2, e=2),
+                in_=sc_b[:, ks].rearrange("p (q u e) -> p u q e", u=2, e=2),
+            )
+        xg_t = {}
+        x_banks = ("tp", "acc", "ot", "acc")
+        for n in range(B * TB + 1):
+            if n < B * TB:
+                xg_t[n] = turn(x_sb[n // TB][:, n % TB, :].bitcast(F32), False, "xg", x_banks[n % 4], n % 2 == 1)
+            if n >= 1:
+                b, t = (n - 1) // TB, (n - 1) % TB
+                xg = xg_t[n - 1]
+                for g in range(G):
+                    cols = slice(t * P, (t + 1) * P)
+                    nc.vector.quantize_mx(
+                        out=xc[:, g, b, cols].bitcast(FP8X4), scales=xs[:, g, b, cols], in_=xg[:, g * 512 : (g + 1) * 512]
+                    )
+        stage_b(0)
+        stage_b(1)
+        stage_c(0)
+
+        for i in range(ON_VECTOR, 5):
+            stage_a(i)
+
+        for i in range(NH + 2):
+            if i + 1 < NH:
+                stage_c(i + 1)
+            v_head = i < NH and order[i][0] == 2
+            if v_head:
+                stage_d(i)
+            if i + 2 < NH:
+                stage_b(i + 2)
+            if i < NH and not v_head:
+                stage_d(i)
+            if i == 0:
+                tables()
+            if 0 <= i - 1 < NH:
+                stage_e(i - 1)
+            if 0 <= i - 2:
+                stage_f(i - 2)
+            if i + 5 < NH:
+                stage_a(i + 5)

@@ -34,34 +34,51 @@ def tile_causalselfattention_pa_kernel(
         keep = ctx.enter_context(tc.tile_pool(name="keep", bufs=1))
         work = ctx.enter_context(tc.tile_pool(name="work", bufs=3))
         psum = ctx.enter_context(tc.psum_pool(name="psum", bufs=2))
-        ctx.enter_context(tc.manual_schedule(engines={mybir.EngineType.PE}))
+        ctx.enter_context(tc.manual_schedule())
 
         ident = keep.tile([P, P], F32, name="ident")
         make_identity(nc, ident[:])
         perm = keep.tile([P, P], F32, name="perm")
         nc.vector.tensor_copy(out=perm[:, 0:64], in_=ident[:, 64:128])
         nc.vector.tensor_copy(out=perm[:, 64:128], in_=ident[:, 0:64])
+        ident_bf = keep.tile([P, P], BF16, name="ident_bf")
+        make_identity(nc, ident_bf[:])
+        sign = keep.tile([P, 1], F32, name="sign")
+        nc.vector.memset(sign[0:64, :], 1.0)
+        nc.vector.memset(sign[64:128, :], -1.0)
         b_rows = keep.tile([P, P], BF16, name="b_rows")
         nc.vector.memset(b_rows[:], 0.0)
+        ones = keep.tile([P, P], BF16, name="ones")
+        nc.gpsimd.memset(ones[:], 1.0)
+        bv_row = keep.tile([P, H * HD], BF16, name="bv_row")
+        nc.gpsimd.memset(bv_row[:], 0.0)
 
+        s_col = keep.tile([P, 8], F32, name="s_col")
         sc_b = keep.tile([P, D], F32, name="sc_b")
-        nc.sync.dma_start(out=sc_b[:], in_=qkv_w_scale.rearrange("o k -> (o k)").partition_broadcast(P))
         w_view = qkv_w_bytes.rearrange("(j h p) k -> h p j k", j=3, h=H, p=P)
         wbytes = [keep.tile([P, 3, D], U8, name="wbytes%d" % h) for h in range(H)]
-        nc.sync.dma_start(out=wbytes[0][:], in_=w_view[0])
         x_sb = [keep.tile([P, TB, D], BF16, name="x_sb%d" % b) for b in range(B)]
         cos_sb = keep.tile([P, TB, HD], BF16, name="cos_sb")
         sin_sb = keep.tile([P, TB, HD], BF16, name="sin_sb")
-        bv = keep.tile([P, H * HD], BF16, name="bv")
-        for b in range(B):
+        bv = keep.tile([P, H * HD], F32, name="bv")
+
+        def load_x(b):
             xv = x[b].rearrange("(p t) k -> p t k", t=TB)
             for t in range(TB):
                 nc.sync.dma_start(out=x_sb[b][:, t, :], in_=xv[:, t, :])
+
+        sin_view = rope_sin[0, 0].rearrange("(p t) d -> p t d", t=TB)
+        nc.sync.dma_start(out=s_col[:], in_=qkv_w_scale.rearrange("o (p c) -> (o p) c", c=8))
+        nc.sync.dma_start(out=wbytes[0][:, 0:1, :], in_=w_view[0][:, 0:1, :])
+        load_x(0)
+        nc.sync.dma_start(out=wbytes[0][:, 1:3, :], in_=w_view[0][:, 1:3, :])
         nc.sync.dma_start(out=cos_sb[:], in_=rope_cos[0, 0].rearrange("(p t) d -> p t d", t=TB))
-        nc.sync.dma_start(out=sin_sb[:], in_=rope_sin[0, 0].rearrange("(p t) d -> p t d", t=TB))
+        nc.sync.dma_start(out=sin_sb[:, :, 0:64], in_=sin_view[:, :, 64:128])
+        nc.sync.dma_start(out=sin_sb[:, :, 64:128], in_=sin_view[:, :, 0:64])
         nc.sync.dma_start(out=b_rows[0:NH, :], in_=qkv_b.rearrange("(r d) -> r d", d=HD))
+        load_x(1)
         nc.sync.dma_start(out=wbytes[1][:], in_=w_view[1])
-        nc.sync.dma_start(out=bv[:], in_=qkv_b[2 * H * HD : 3 * H * HD].partition_broadcast(P))
+        nc.sync.dma_start(out=bv_row[0:1, :], in_=qkv_b[2 * H * HD : 3 * H * HD].rearrange("(o n) -> o n", o=1))
         for h in range(2, H):
             nc.sync.dma_start(out=wbytes[h][:], in_=w_view[h])
 
@@ -73,21 +90,18 @@ def tile_causalselfattention_pa_kernel(
         def bank(tag):
             return psum.tile([P, TB, P], F32, name=tag, tag=tag, bufs=(4 if tag == "acc" else 2))
 
-        def turn(words, sorted_words, name, tag, on_vector):
+        def turn(words, sorted_words, dst, tag, on_vector):
             tp = bank(tag)
             for g in range(G):
                 for u in range(2):
                     n = 2 * g + u
                     picked = words[:, P * n : P * (n + 1)] if sorted_words else words[:, 256 * g + u : 256 * (g + 1) : 2]
                     nc.tensor.transpose(tp[:, n, :], picked, ident[:])
-            grouped = work.tile([P, G * 512], BF16, name=name, tag=name, bufs=3, align_bytes=64)
-            dst = grouped[:].bitcast(F32).rearrange("p (g r u) -> p g r u", g=G, u=2)
             src = tp[:].rearrange("p (g u) r -> p g r u", g=G)
             if on_vector:
                 nc.vector.tensor_copy(out=dst, in_=src)
             else:
                 nc.scalar.copy(out=dst, in_=src)
-            return grouped
 
         wb_t = {}
         wg_t = {}
@@ -108,13 +122,15 @@ def tile_causalselfattention_pa_kernel(
                     nc.gpsimd.tensor_tensor(
                         out=wb[:, ks].rearrange("p (u q e) -> p u q e", u=2, e=2),
                         in0=wf[:, ks].rearrange("p (q u e) -> p u q e", u=2, e=2),
-                        in1=sc_p[:, ks].rearrange("p (u q e) -> p u q e", u=2, e=2),
+                        in1=sc_b[:, ks].rearrange("p (q u e) -> p u q e", u=2, e=2),
                         op=MULT,
                     )
             wb_t[i] = wb
 
         def stage_b(i):
-            wg_t[i] = turn(wb_t[i][:].bitcast(F32), i >= ON_VECTOR, "wg", "tp", False)
+            wg_t[i] = work.tile([P, G * 512], BF16, name="wg", tag="wg", bufs=3, align_bytes=64)
+            dst = wg_t[i][:].bitcast(F32).rearrange("p (g r u) -> p g r u", g=G, u=2)
+            turn(wb_t[i][:].bitcast(F32), i >= ON_VECTOR, dst, "tp", False)
 
         def stage_c(i):
             nc.vector.quantize_mx(out=wc[:, i, :].bitcast(FP8X4), scales=ws[:, i, :], in_=wg_t[i][:])
@@ -194,53 +210,61 @@ def tile_causalselfattention_pa_kernel(
                 nc.scalar.copy(out=o_sb[:], in_=ot[:])
                 store(j, h, b, o_sb[:].rearrange("p t d -> p (t d)"))
 
-        cos_f = keep.tile([P, TB, HD], F32, name="cos_f")
-        sin_p = keep.tile([P, TB, HD], F32, name="sin_p")
-        b_f = keep.tile([P, P], F32, name="b_f")
         tab = keep.tile([P, 2, T], F32, name="tab")
         bcol = keep.tile([P, P], F32, name="bcol")
 
+        def bank_bf(tag):
+            return psum.tile([P, TB, P], BF16, name=tag + "_bf", tag=tag, bufs=2)
+
         def tables():
-            nc.scalar.copy(out=cos_f[:], in_=cos_sb[:])
-            nc.scalar.copy(out=sin_p[:, :, 0:64], in_=sin_sb[:, :, 64:128])
-            nc.scalar.activation(out=sin_p[:, :, 64:128], in_=sin_sb[:, :, 0:64], func=COPY, scale=-1.0)
-            nc.scalar.copy(out=b_f[:], in_=b_rows[:])
-            for n, src in enumerate((cos_f, sin_p)):
+            cos_t = bank_bf("ot")
+            for t in range(TB):
+                nc.tensor.transpose(cos_t[:, t, :], cos_sb[:, t, :], ident_bf[:])
+            nc.scalar.copy(out=tab[:, 0, :], in_=cos_t[:].rearrange("p t r -> p (t r)"))
+            sin_t = bank_bf("ot")
+            for t in range(TB):
+                nc.tensor.transpose(sin_t[:, t, :], sin_sb[:, t, :], ident_bf[:])
+            nc.scalar.activation(out=tab[:, 1, :], in_=sin_t[:].rearrange("p t r -> p (t r)"), func=COPY, scale=sign[:, 0:1])
+            b_t = bank_bf("tp")
+            nc.tensor.transpose(b_t[:, 0, :], b_rows[:], ident_bf[:])
+            nc.scalar.copy(out=bcol[:], in_=b_t[:, 0, :])
+
+        def spread_v_bias():
+            for n in range(2):
                 tp = bank("tp")
-                for t in range(TB):
-                    nc.tensor.transpose(tp[:, t, :], src[:, t, :], ident[:])
-                nc.scalar.copy(out=tab[:, n, :], in_=tp[:].rearrange("p t r -> p (t r)"))
-            tp = bank("tp")
-            nc.tensor.transpose(tp[:, 0, :], b_f[:], ident[:])
-            nc.scalar.copy(out=bcol[:], in_=tp[:, 0, :])
+                flat = tp[:].rearrange("p t r -> p (t r)")
+                nc.tensor.matmul(flat, lhsT=ones[:], rhs=bv_row[:, n * 512 : (n + 1) * 512], start=True, stop=True)
+                nc.scalar.copy(out=bv[:, n * 512 : (n + 1) * 512], in_=flat)
 
-        for i in range(ON_VECTOR):
-            stage_a(i)
-        sc_p = keep.tile([P, D], F32, name="sc_p")
-        for g in range(G):
-            ks = slice(g * 512, (g + 1) * 512)
-            nc.vector.tensor_copy(
-                out=sc_p[:, ks].rearrange("p (u q e) -> p u q e", u=2, e=2),
-                in_=sc_b[:, ks].rearrange("p (q u e) -> p u q e", u=2, e=2),
-            )
-        xg_t = {}
-        x_banks = ("tp", "acc", "ot", "acc")
-        for n in range(B * TB + 1):
-            if n < B * TB:
-                xg_t[n] = turn(x_sb[n // TB][:, n % TB, :].bitcast(F32), False, "xg", x_banks[n % 4], n % 2 == 1)
-            if n >= 1:
-                b, t = (n - 1) // TB, (n - 1) % TB
-                xg = xg_t[n - 1]
-                for g in range(G):
-                    cols = slice(t * P, (t + 1) * P)
-                    nc.vector.quantize_mx(
-                        out=xc[:, g, b, cols].bitcast(FP8X4), scales=xs[:, g, b, cols], in_=xg[:, g * 512 : (g + 1) * 512]
-                    )
+        for c2 in range(2):
+            sp = bank("ot")
+            for c in range(4):
+                nc.tensor.transpose(sp[:, c, :], s_col[:, 4 * c2 + c : 4 * c2 + c + 1].to_broadcast([P, P]), ident[:])
+            dst = sc_b[:].rearrange("p (n a c) -> p a n c", a=2, c=4)[:, c2]
+            src = sp[:].rearrange("p c n -> p n c")
+            if c2 == 0:
+                nc.vector.tensor_copy(out=dst, in_=src)
+            else:
+                nc.scalar.copy(out=dst, in_=src)
+        xg = [keep.tile([P, G, 4 * T], BF16, name="xg%d" % b, align_bytes=64) for b in range(B)]
+
+        def x_road(b):
+            for t in range(TB):
+                dst = xg[b][:].rearrange("p g c -> p (g c)").bitcast(F32).rearrange("p (g r u) -> p g r u", g=G, u=2)
+                turn(x_sb[b][:, t, :].bitcast(F32), False, dst[:, :, t * P : (t + 1) * P, :], ("tp", "acc")[t % 2], t % 2 == 1)
+            for g in range(G):
+                nc.vector.quantize_mx(out=xc[:, g, b, :].bitcast(FP8X4), scales=xs[:, g, b, :], in_=xg[b][:, g, :])
+
+        stage_a(0)
+        x_road(0)
         stage_b(0)
-        stage_b(1)
         stage_c(0)
-
-        for i in range(ON_VECTOR, 5):
+        for i in range(1, 3):
+            stage_a(i)
+        tables()
+        x_road(1)
+        stage_b(1)
+        for i in range(3, 5):
             stage_a(i)
 
         for i in range(NH + 2):
@@ -253,8 +277,8 @@ def tile_causalselfattention_pa_kernel(
                 stage_b(i + 2)
             if i < NH and not v_head:
                 stage_d(i)
-            if i == 0:
-                tables()
+            if i == 1:
+                spread_v_bias()
             if 0 <= i - 1 < NH:
                 stage_e(i - 1)
             if 0 <= i - 2:

@@ -88,7 +88,7 @@ def tile_causalselfattention_pa_kernel(
         ws = keep.tile([P, NH, G * P], U8, name="ws", align_bytes=64)
 
         def bank(tag):
-            return psum.tile([P, TB, P], F32, name=tag, tag=tag, bufs=(4 if tag == "acc" else 2))
+            return psum.tile([P, TB, P], F32, name=tag, tag=tag, bufs=4)
 
         def turn(words, sorted_words, dst, tag, on_vector):
             tp = bank(tag)
@@ -130,7 +130,7 @@ def tile_causalselfattention_pa_kernel(
         def stage_b(i):
             wg_t[i] = work.tile([P, G * 512], BF16, name="wg", tag="wg", bufs=3, align_bytes=64)
             dst = wg_t[i][:].bitcast(F32).rearrange("p (g r u) -> p g r u", g=G, u=2)
-            turn(wb_t[i][:].bitcast(F32), i >= ON_VECTOR, dst, "tp", False)
+            turn(wb_t[i][:].bitcast(F32), i >= ON_VECTOR, dst, "tr", False)
 
         def stage_c(i):
             nc.vector.quantize_mx(out=wc[:, i, :].bitcast(FP8X4), scales=ws[:, i, :], in_=wg_t[i][:])
@@ -175,7 +175,7 @@ def tile_causalselfattention_pa_kernel(
             for b in range(B):
                 acc = acc_t[(i, b)]
                 if j == 2:
-                    o_sb = work.tile([P, TB, HD], F32, name="o_sb", tag="o_sb", bufs=4)
+                    o_sb = work.tile([P, TB, HD], F32, name="o_sb", tag="o_sb", bufs=8)
                     nc.vector.tensor_tensor(
                         out=o_sb[:],
                         in0=acc[:],
@@ -201,12 +201,12 @@ def tile_causalselfattention_pa_kernel(
                 return
             for b in range(B):
                 ar = ar_t[(i, b)]
-                ot = bank("ot")
+                ot = bank("tr")
                 for t in range(TB):
                     cols = slice(t * P, (t + 1) * P)
                     nc.tensor.matmul(ot[:, t, :], lhsT=ar[:, 0, cols], rhs=ident[:], start=True, stop=False, is_transpose=True)
                     nc.tensor.matmul(ot[:, t, :], lhsT=ar[:, 1, cols], rhs=perm[:], start=False, stop=True, is_transpose=True)
-                o_sb = work.tile([P, TB, HD], F32, name="o_sb", tag="o_sb", bufs=4)
+                o_sb = work.tile([P, TB, HD], F32, name="o_sb", tag="o_sb", bufs=8)
                 nc.scalar.copy(out=o_sb[:], in_=ot[:])
                 store(j, h, b, o_sb[:].rearrange("p t d -> p (t d)"))
 
@@ -214,30 +214,30 @@ def tile_causalselfattention_pa_kernel(
         bcol = keep.tile([P, P], F32, name="bcol")
 
         def bank_bf(tag):
-            return psum.tile([P, TB, P], BF16, name=tag + "_bf", tag=tag, bufs=2)
+            return psum.tile([P, TB, P], BF16, name=tag + "_bf", tag=tag, bufs=4)
 
         def tables():
-            cos_t = bank_bf("ot")
+            cos_t = bank_bf("tr")
             for t in range(TB):
                 nc.tensor.transpose(cos_t[:, t, :], cos_sb[:, t, :], ident_bf[:])
             nc.scalar.copy(out=tab[:, 0, :], in_=cos_t[:].rearrange("p t r -> p (t r)"))
-            sin_t = bank_bf("ot")
+            sin_t = bank_bf("tr")
             for t in range(TB):
                 nc.tensor.transpose(sin_t[:, t, :], sin_sb[:, t, :], ident_bf[:])
             nc.scalar.activation(out=tab[:, 1, :], in_=sin_t[:].rearrange("p t r -> p (t r)"), func=COPY, scale=sign[:, 0:1])
-            b_t = bank_bf("tp")
+            b_t = bank_bf("tr")
             nc.tensor.transpose(b_t[:, 0, :], b_rows[:], ident_bf[:])
             nc.scalar.copy(out=bcol[:], in_=b_t[:, 0, :])
 
         def spread_v_bias():
             for n in range(2):
-                tp = bank("tp")
+                tp = bank("tr")
                 flat = tp[:].rearrange("p t r -> p (t r)")
                 nc.tensor.matmul(flat, lhsT=ones[:], rhs=bv_row[:, n * 512 : (n + 1) * 512], start=True, stop=True)
                 nc.scalar.copy(out=bv[:, n * 512 : (n + 1) * 512], in_=flat)
 
         for c2 in range(2):
-            sp = bank("ot")
+            sp = bank("tr")
             for c in range(4):
                 nc.tensor.transpose(sp[:, c, :], s_col[:, 4 * c2 + c : 4 * c2 + c + 1].to_broadcast([P, P]), ident[:])
             dst = sc_b[:].rearrange("p (n a c) -> p a n c", a=2, c=4)[:, c2]
@@ -251,7 +251,7 @@ def tile_causalselfattention_pa_kernel(
         def x_road(b):
             for t in range(TB):
                 dst = xg[b][:].rearrange("p g c -> p (g c)").bitcast(F32).rearrange("p (g r u) -> p g r u", g=G, u=2)
-                turn(x_sb[b][:, t, :].bitcast(F32), False, dst[:, :, t * P : (t + 1) * P, :], ("tp", "acc")[t % 2], t % 2 == 1)
+                turn(x_sb[b][:, t, :].bitcast(F32), False, dst[:, :, t * P : (t + 1) * P, :], "acc", t % 2 == 1)
             for g in range(G):
                 nc.vector.quantize_mx(out=xc[:, g, b, :].bitcast(FP8X4), scales=xs[:, g, b, :], in_=xg[b][:, g, :])
 
@@ -263,13 +263,13 @@ def tile_causalselfattention_pa_kernel(
             stage_a(i)
         tables()
         x_road(1)
-        stage_b(1)
         for i in range(3, 5):
             stage_a(i)
+        stage_b(1)
 
         for i in range(NH + 2):
-            if i + 1 < NH:
-                stage_c(i + 1)
+            if i + 5 < NH:
+                stage_a(i + 5)
             v_head = i < NH and order[i][0] == 2
             if v_head:
                 stage_d(i)
@@ -277,11 +277,11 @@ def tile_causalselfattention_pa_kernel(
                 stage_b(i + 2)
             if i < NH and not v_head:
                 stage_d(i)
-            if i == 1:
-                spread_v_bias()
             if 0 <= i - 1 < NH:
                 stage_e(i - 1)
+            if i + 1 < NH:
+                stage_c(i + 1)
             if 0 <= i - 2:
                 stage_f(i - 2)
-            if i + 5 < NH:
-                stage_a(i + 5)
+            if i == 1:
+                spread_v_bias()

@@ -20,7 +20,8 @@ P = 128
 G = D // 512
 TB = T // P
 NH = 3 * H
-ON_VECTOR = 3
+def on_vector(i):
+    return i < 3 or i % 6 == 1
 
 
 def tile_causalselfattention_pa_kernel(
@@ -112,7 +113,7 @@ def tile_causalselfattention_pa_kernel(
             j, h = order[i]
             codes = wbytes[h][:, j, :].bitcast(FP8)
             wb = work.tile([P, D], BF16, name="wb", tag="wb", bufs=4, align_bytes=64)
-            if i < ON_VECTOR:
+            if on_vector(i):
                 nc.vector.tensor_tensor(out=wb[:], in0=codes, in1=sc_b[:], op=MULT)
             else:
                 wf = work.tile([P, D], BF16, name="wf", tag="wf", bufs=3)
@@ -130,7 +131,7 @@ def tile_causalselfattention_pa_kernel(
         def stage_b(i):
             wg_t[i] = work.tile([P, G * 512], BF16, name="wg", tag="wg", bufs=3, align_bytes=64)
             dst = wg_t[i][:].bitcast(F32).rearrange("p (g r u) -> p g r u", g=G, u=2)
-            turn(wb_t[i][:].bitcast(F32), i >= ON_VECTOR, dst, "tr", False)
+            turn(wb_t[i][:].bitcast(F32), not on_vector(i), dst, "tr", False)
 
         def stage_c(i):
             nc.vector.quantize_mx(out=wc[:, i, :].bitcast(FP8X4), scales=ws[:, i, :], in_=wg_t[i][:])

@@ -118,20 +118,13 @@ def tile_causalselfattention_pa_kernel(
             else:
                 wf = work.tile([P, D], BF16, name="wf", tag="wf", bufs=3)
                 nc.scalar.copy(out=wf[:], in_=codes)
-                for g in range(G):
-                    ks = slice(g * 512, (g + 1) * 512)
-                    nc.gpsimd.tensor_tensor(
-                        out=wb[:, ks].rearrange("p (u q e) -> p u q e", u=2, e=2),
-                        in0=wf[:, ks].rearrange("p (q u e) -> p u q e", u=2, e=2),
-                        in1=sc_b[:, ks].rearrange("p (q u e) -> p u q e", u=2, e=2),
-                        op=MULT,
-                    )
+                nc.gpsimd.tensor_tensor(out=wb[:], in0=wf[:], in1=sc_b[:], op=MULT)
             wb_t[i] = wb
 
         def stage_b(i):
             wg_t[i] = work.tile([P, G * 512], BF16, name="wg", tag="wg", bufs=3, align_bytes=64)
             dst = wg_t[i][:].bitcast(F32).rearrange("p (g r u) -> p g r u", g=G, u=2)
-            turn(wb_t[i][:].bitcast(F32), not on_vector(i), dst, "tr", False)
+            turn(wb_t[i][:].bitcast(F32), False, dst, "tr", False)
 
         def stage_c(i):
             nc.vector.quantize_mx(out=wc[:, i, :].bitcast(FP8X4), scales=ws[:, i, :], in_=wg_t[i][:])

@@ -21,7 +21,7 @@ G = D // 512
 TB = T // P
 NH = 3 * H
 def on_vector(i):
-    return i < 3 or i % 6 == 1
+    return i < 3
 
 
 def tile_causalselfattention_pa_kernel(

@@ -70,15 +70,14 @@ def tile_causalselfattention_pa_kernel(
 
         sin_view = rope_sin[0, 0].rearrange("(p t) d -> p t d", t=TB)
         nc.sync.dma_start(out=s_col[:], in_=qkv_w_scale.rearrange("o (p c) -> (o p) c", c=8))
-        nc.sync.dma_start(out=wbytes[0][:, 0:1, :], in_=w_view[0][:, 0:1, :])
+        nc.sync.dma_start(out=wbytes[0][:], in_=w_view[0])
         load_x(0)
-        nc.sync.dma_start(out=wbytes[0][:, 1:3, :], in_=w_view[0][:, 1:3, :])
         nc.sync.dma_start(out=cos_sb[:], in_=rope_cos[0, 0].rearrange("(p t) d -> p t d", t=TB))
         nc.sync.dma_start(out=sin_sb[:, :, 0:64], in_=sin_view[:, :, 64:128])
         nc.sync.dma_start(out=sin_sb[:, :, 64:128], in_=sin_view[:, :, 0:64])
         nc.sync.dma_start(out=b_rows[0:NH, :], in_=qkv_b.rearrange("(r d) -> r d", d=HD))
-        load_x(1)
         nc.sync.dma_start(out=wbytes[1][:], in_=w_view[1])
+        load_x(1)
         nc.sync.dma_start(out=bv_row[0:1, :], in_=qkv_b[2 * H * HD : 3 * H * HD].rearrange("(o n) -> o n", o=1))
         for h in range(2, H):
             nc.sync.dma_start(out=wbytes[h][:], in_=w_view[h])
@@ -245,7 +244,7 @@ def tile_causalselfattention_pa_kernel(
         def x_road(b):
             for t in range(TB):
                 dst = xg[b][:].rearrange("p g c -> p (g c)").bitcast(F32).rearrange("p (g r u) -> p g r u", g=G, u=2)
-                turn(x_sb[b][:, t, :].bitcast(F32), False, dst[:, :, t * P : (t + 1) * P, :], "acc", t % 2 == 1)
+                turn(x_sb[b][:, t, :].bitcast(F32), False, dst[:, :, t * P : (t + 1) * P, :], "acc", t % 2 == 1 if b == 1 else t == TB - 1)
             for g in range(G):
                 nc.vector.quantize_mx(out=xc[:, g, b, :].bitcast(FP8X4), scales=xs[:, g, b, :], in_=xg[b][:, g, :])
 
@@ -256,9 +255,9 @@ def tile_causalselfattention_pa_kernel(
         for i in range(1, 3):
             stage_a(i)
         tables()
+        stage_a(3)
         x_road(1)
-        for i in range(3, 5):
-            stage_a(i)
+        stage_a(4)
         stage_b(1)
 
         for i in range(NH + 2):

from contextlib import ExitStack

import concourse.mybir as mybir
from concourse.masks import make_identity

B, T, D, H, HD = 2, 512, 1024, 8, 128
FLOPS = 2 * B * T * D * 3 * H * HD

F32 = mybir.dt.float32
BF16 = mybir.dt.bfloat16
U32 = mybir.dt.uint32
U8 = mybir.dt.uint8
FP8 = mybir.dt.float8_e4m3fn
FP8X4 = mybir.dt.float8_e4m3fn_x4
ADD = mybir.AluOpType.add
MULT = mybir.AluOpType.mult
COPY = mybir.ActivationFunctionType.Copy

P = 128
G = D // 512
TB = T // P
NH = 3 * H
def on_vector(i):
    return i < 3


def tile_causalselfattention_pa_kernel(
    tc, x, rope_cos, rope_sin, qkv_w_bytes, qkv_w_scale, qkv_b, out_0, out_1, out_2
):
    nc = tc.nc
    outs = (out_0, out_1, out_2)
    order = [(j, h) for h in range(H) for j in range(3)]

    with ExitStack() as ctx:
        keep = ctx.enter_context(tc.tile_pool(name="keep", bufs=1))
        work = ctx.enter_context(tc.tile_pool(name="work", bufs=3))
        psum = ctx.enter_context(tc.psum_pool(name="psum", bufs=2))
        ctx.enter_context(tc.manual_schedule())

        ident = keep.tile([P, P], F32, name="ident")
        make_identity(nc, ident[:])
        perm = keep.tile([P, P], F32, name="perm")
        nc.vector.tensor_copy(out=perm[:, 0:64], in_=ident[:, 64:128])
        nc.vector.tensor_copy(out=perm[:, 64:128], in_=ident[:, 0:64])
        ident_bf = keep.tile([P, P], BF16, name="ident_bf")
        make_identity(nc, ident_bf[:])
        sign = keep.tile([P, 1], F32, name="sign")
        nc.vector.memset(sign[0:64, :], 1.0)
        nc.vector.memset(sign[64:128, :], -1.0)
        b_rows = keep.tile([P, P], BF16, name="b_rows")
        nc.vector.memset(b_rows[:], 0.0)
        ones = keep.tile([P, P], BF16, name="ones")
        nc.gpsimd.memset(ones[:], 1.0)
        bv_row = keep.tile([P, H * HD], BF16, name="bv_row")
        nc.gpsimd.memset(bv_row[:], 0.0)

        s_col = keep.tile([P, 8], F32, name="s_col")
        sc_b = keep.tile([P, D], F32, name="sc_b")
        w_view = qkv_w_bytes.rearrange("(j h p) k -> h p j k", j=3, h=H, p=P)
        wbytes = [keep.tile([P, 3, D], U8, name="wbytes%d" % h) for h in range(H)]
        x_sb = [keep.tile([P, TB, D], BF16, name="x_sb%d" % b) for b in range(B)]
        cos_sb = keep.tile([P, TB, HD], BF16, name="cos_sb")
        sin_sb = keep.tile([P, TB, HD], BF16, name="sin_sb")
        bv = keep.tile([P, H * HD], F32, name="bv")

        def load_x(b):
            xv = x[b].rearrange("(p t) k -> p t k", t=TB)
            for t in range(TB):
                nc.sync.dma_start(out=x_sb[b][:, t, :], in_=xv[:, t, :])

        sin_view = rope_sin[0, 0].rearrange("(p t) d -> p t d", t=TB)
        nc.sync.dma_start(out=s_col[:], in_=qkv_w_scale.rearrange("o (p c) -> (o p) c", c=8))
        nc.sync.dma_start(out=wbytes[0][:], in_=w_view[0])
        load_x(0)
        nc.sync.dma_start(out=cos_sb[:], in_=rope_cos[0, 0].rearrange("(p t) d -> p t d", t=TB))
        nc.sync.dma_start(out=sin_sb[:, :, 0:64], in_=sin_view[:, :, 64:128])
        nc.sync.dma_start(out=sin_sb[:, :, 64:128], in_=sin_view[:, :, 0:64])
        nc.sync.dma_start(out=b_rows[0:NH, :], in_=qkv_b.rearrange("(r d) -> r d", d=HD))
        nc.sync.dma_start(out=wbytes[1][:], in_=w_view[1])
        load_x(1)
        nc.sync.dma_start(out=bv_row[0:1, :], in_=qkv_b[2 * H * HD : 3 * H * HD].rearrange("(o n) -> o n", o=1))
        for h in range(2, H):
            nc.sync.dma_start(out=wbytes[h][:], in_=w_view[h])

        xc = keep.tile([P, G, B, T], U32, name="xc", align_bytes=64)
        xs = keep.tile([P, G, B, T], U8, name="xs", align_bytes=64)
        wc = keep.tile([P, NH, G * P], U32, name="wc", align_bytes=64)
        ws = keep.tile([P, NH, G * P], U8, name="ws", align_bytes=64)

        def bank(tag):
            return psum.tile([P, TB, P], F32, name=tag, tag=tag, bufs=4)

        def turn(words, sorted_words, dst, tag, on_vector):
            tp = bank(tag)
            for g in range(G):
                for u in range(2):
                    n = 2 * g + u
                    picked = words[:, P * n : P * (n + 1)] if sorted_words else words[:, 256 * g + u : 256 * (g + 1) : 2]
                    nc.tensor.transpose(tp[:, n, :], picked, ident[:])
            src = tp[:].rearrange("p (g u) r -> p g r u", g=G)
            if on_vector:
                nc.vector.tensor_copy(out=dst, in_=src)
            else:
                nc.scalar.copy(out=dst, in_=src)

        wb_t = {}
        wg_t = {}
        acc_t = {}
        ar_t = {}

        def stage_a(i):
            j, h = order[i]
            codes = wbytes[h][:, j, :].bitcast(FP8)
            wb = work.tile([P, D], BF16, name="wb", tag="wb", bufs=4, align_bytes=64)
            if on_vector(i):
                nc.vector.tensor_tensor(out=wb[:], in0=codes, in1=sc_b[:], op=MULT)
            else:
                wf = work.tile([P, D], BF16, name="wf", tag="wf", bufs=3)
                nc.scalar.copy(out=wf[:], in_=codes)
                nc.gpsimd.tensor_tensor(out=wb[:], in0=wf[:], in1=sc_b[:], op=MULT)
            wb_t[i] = wb

        def stage_b(i):
            wg_t[i] = work.tile([P, G * 512], BF16, name="wg", tag="wg", bufs=3, align_bytes=64)
            dst = wg_t[i][:].bitcast(F32).rearrange("p (g r u) -> p g r u", g=G, u=2)
            turn(wb_t[i][:].bitcast(F32), False, dst, "tr", False)

        def stage_c(i):
            nc.vector.quantize_mx(out=wc[:, i, :].bitcast(FP8X4), scales=ws[:, i, :], in_=wg_t[i][:])

        def stage_d(i):
            j, h = order[i]
            for b in range(B):
                acc = bank("acc")
                if j == 2:
                    for t in range(TB):
                        toks = slice(t * P, (t + 1) * P)
                        for g in range(G):
                            cols = slice(g * P, (g + 1) * P)
                            nc.tensor.matmul_mx(
                                out=acc[:, t, :],
                                lhsT=xc[:, g, b, toks].bitcast(FP8X4),
                                lhsT_scale=xs[:, g, b, toks],
                                rhs=wc[:, i, cols].bitcast(FP8X4),
                                rhs_scale=ws[:, i, cols],
                                start=(g == 0),
                                stop=(g == G - 1),
                            )
                else:
                    for g in range(G):
                        cols = slice(g * P, (g + 1) * P)
                        nc.tensor.matmul_mx(
                            out=acc[:].rearrange("p t r -> p (t r)"),
                            lhsT=wc[:, i, cols].bitcast(FP8X4),
                            lhsT_scale=ws[:, i, cols],
                            rhs=xc[:, g, b, :].bitcast(FP8X4),
                            rhs_scale=xs[:, g, b, :],
                            start=(g == 0),
                            stop=(g == G - 1),
                        )
                acc_t[(i, b)] = acc

        def store(j, h, b, o_sb):
            nc.sync.dma_start(out=outs[j][b, h].rearrange("(p t) d -> p (t d)", t=TB), in_=o_sb)

        def stage_e(i):
            j, h = order[i]
            for b in range(B):
                acc = acc_t[(i, b)]
                if j == 2:
                    o_sb = work.tile([P, TB, HD], F32, name="o_sb", tag="o_sb", bufs=8)
                    nc.vector.tensor_tensor(
                        out=o_sb[:],
                        in0=acc[:],
                        in1=bv[:, h * HD : (h + 1) * HD].unsqueeze(1).to_broadcast([P, TB, HD]),
                        op=ADD,
                    )
                    store(j, h, b, o_sb[:].rearrange("p t d -> p (t d)"))
                else:
                    ar = work.tile([P, 2, T], F32, name="ar", tag="ar", bufs=4)
                    nc.vector.scalar_tensor_tensor(
                        out=ar[:],
                        in0=acc[:].rearrange("p t r -> p (t r)").unsqueeze(1).to_broadcast([P, 2, T]),
                        scalar=bcol[:, j * H + h : j * H + h + 1],
                        in1=tab[:],
                        op0=ADD,
                        op1=MULT,
                    )
                    ar_t[(i, b)] = ar

        def stage_f(i):
            j, h = order[i]
            if j == 2:
                return
            for b in range(B):
                ar = ar_t[(i, b)]
                ot = bank("tr")
                for t in range(TB):
                    cols = slice(t * P, (t + 1) * P)
                    nc.tensor.matmul(ot[:, t, :], lhsT=ar[:, 0, cols], rhs=ident[:], start=True, stop=False, is_transpose=True)
                    nc.tensor.matmul(ot[:, t, :], lhsT=ar[:, 1, cols], rhs=perm[:], start=False, stop=True, is_transpose=True)
                o_sb = work.tile([P, TB, HD], F32, name="o_sb", tag="o_sb", bufs=8)
                nc.scalar.copy(out=o_sb[:], in_=ot[:])
                store(j, h, b, o_sb[:].rearrange("p t d -> p (t d)"))

        tab = keep.tile([P, 2, T], F32, name="tab")
        bcol = keep.tile([P, P], F32, name="bcol")

        def bank_bf(tag):
            return psum.tile([P, TB, P], BF16, name=tag + "_bf", tag=tag, bufs=4)

        def tables():
            cos_t = bank_bf("tr")
            for t in range(TB):
                nc.tensor.transpose(cos_t[:, t, :], cos_sb[:, t, :], ident_bf[:])
            nc.scalar.copy(out=tab[:, 0, :], in_=cos_t[:].rearrange("p t r -> p (t r)"))
            sin_t = bank_bf("tr")
            for t in range(TB):
                nc.tensor.transpose(sin_t[:, t, :], sin_sb[:, t, :], ident_bf[:])
            nc.scalar.activation(out=tab[:, 1, :], in_=sin_t[:].rearrange("p t r -> p (t r)"), func=COPY, scale=sign[:, 0:1])
            b_t = bank_bf("tr")
            nc.tensor.transpose(b_t[:, 0, :], b_rows[:], ident_bf[:])
            nc.scalar.copy(out=bcol[:], in_=b_t[:, 0, :])

        def spread_v_bias():
            for n in range(2):
                tp = bank("tr")
                flat = tp[:].rearrange("p t r -> p (t r)")
                nc.tensor.matmul(flat, lhsT=ones[:], rhs=bv_row[:, n * 512 : (n + 1) * 512], start=True, stop=True)
                nc.scalar.copy(out=bv[:, n * 512 : (n + 1) * 512], in_=flat)

        for c2 in range(2):
            sp = bank("tr")
            for c in range(4):
                nc.tensor.transpose(sp[:, c, :], s_col[:, 4 * c2 + c : 4 * c2 + c + 1].to_broadcast([P, P]), ident[:])
            dst = sc_b[:].rearrange("p (n a c) -> p a n c", a=2, c=4)[:, c2]
            src = sp[:].rearrange("p c n -> p n c")
            if c2 == 0:
                nc.vector.tensor_copy(out=dst, in_=src)
            else:
                nc.scalar.copy(out=dst, in_=src)
        xg = [keep.tile([P, G, 4 * T], BF16, name="xg%d" % b, align_bytes=64) for b in range(B)]

        def x_road(b):
            for t in range(TB):
                dst = xg[b][:].rearrange("p g c -> p (g c)").bitcast(F32).rearrange("p (g r u) -> p g r u", g=G, u=2)
                turn(x_sb[b][:, t, :].bitcast(F32), False, dst[:, :, t * P : (t + 1) * P, :], "acc", t % 2 == 1 if b == 1 else t == TB - 1)
            for g in range(G):
                nc.vector.quantize_mx(out=xc[:, g, b, :].bitcast(FP8X4), scales=xs[:, g, b, :], in_=xg[b][:, g, :])

        stage_a(0)
        x_road(0)
        stage_b(0)
        stage_c(0)
        for i in range(1, 3):
            stage_a(i)
        tables()
        stage_a(3)
        x_road(1)
        stage_a(4)
        stage_b(1)

        for i in range(NH + 2):
            if i + 5 < NH:
                stage_a(i + 5)
            v_head = i < NH and order[i][0] == 2
            if v_head:
                stage_d(i)
            if i + 2 < NH:
                stage_b(i + 2)
            if i < NH and not v_head:
                stage_d(i)
            if 0 <= i - 1 < NH:
                stage_e(i - 1)
            if i + 1 < NH:
                stage_c(i + 1)
            if 0 <= i - 2:
                stage_f(i - 2)
            if i == 1:
                spread_v_bias()
